import numpy as np
import ml_dtypes

BF16 = ml_dtypes.bfloat16


def bf(x):
    return np.asarray(x, np.float32).astype(BF16)


def f32(x):
    return np.asarray(x, np.float32)


def f64(x):
    return np.asarray(x).astype(np.float64)


def striped(idx):
    return np.tile(idx.reshape(-1, 16).T, (8, 1))


C, S, K, H, A, E, N = 512, 1024, 4, 512, 4, 128, 2048


def setup_inputs():
    return {
        "wtok": f32(np.random.standard_normal((C, S))),
        "wpos": f32(0.75 * np.random.standard_normal((C, H))),
        "wq": bf(np.random.standard_normal((C, C)) / np.sqrt(C)),
        "bq": f32(0.1 * np.random.standard_normal((C, 1))),
        "wk": bf(np.random.standard_normal((C, C)) / np.sqrt(C)),
        "wv": bf(np.random.standard_normal((C, C)) / np.sqrt(C)),
        "bv": f32(0.1 * np.random.standard_normal((C, 1))),
        "offs": striped(np.concatenate([np.random.permutation(S)[:H] for _ in range(K)])),
    }


def reference(wtok, wpos, wq, bq, wk, wv, bv, offs):
    idx = offs[:16].T.reshape(-1)
    x = f64(wtok)[:, idx] + np.tile(f64(wpos), (1, K))
    q = (f64(wq).T @ x + f64(bq)).reshape(A, E, K, H)
    k = (f64(wk).T @ x).reshape(A, E, K, H)
    v = (f64(wv).T @ x + f64(bv)).reshape(A, E, K, H)
    sc = np.einsum("aerq,aeru->arqu", q, k) / np.sqrt(C)
    keep = np.tril(np.ones((H, H), bool))
    e = np.where(keep, np.exp(sc), 0.0)
    p = e / e.sum(axis=-1, keepdims=True)
    return np.einsum("arqu,aeru->aerq", p, v).reshape(C, N)

@@ -1,0 +1,138 @@
+import math
+
+import concourse.mybir as mybir
+from concourse.masks import make_identity
+
+F32 = mybir.dt.float32
+BF16 = mybir.dt.bfloat16
+U16 = mybir.dt.uint16
+ADD = mybir.AluOpType.add
+MAX = mybir.AluOpType.max
+IS_GE = mybir.AluOpType.is_ge
+EXP = mybir.ActivationFunctionType.Exp
+IDENTITY = mybir.ActivationFunctionType.Identity
+X_AXIS = mybir.AxisListType.X
+
+P = 128
+FEATURES = 512
+VOCAB = 1024
+SEQ = 512
+N_SEQ = 4
+N_HEAD = 4
+N_FBLK = FEATURES // P
+N_TBLK = SEQ // P
+SCALE = 1.0 / math.sqrt(FEATURES)
+MASKED = -1.0e9
+
+FLOPS = 3 * 2 * FEATURES * FEATURES * N_SEQ * SEQ + 2 * 2 * P * (SEQ * (SEQ + 1) // 2) * N_HEAD * N_SEQ
+
+
+def tile_thetransformer_b_kernel(tc, wtok, wpos, wq, bq, wk, wv, bv, offs, out):
+    nc = tc.nc
+    with (
+        tc.tile_pool(name="held", bufs=1) as held,
+        tc.tile_pool(name="xpool", bufs=4) as xpool,
+        tc.tile_pool(name="seqpool", bufs=2) as seqpool,
+        tc.tile_pool(name="headpool", bufs=3) as headpool,
+        tc.tile_pool(name="rowpool", bufs=4) as rowpool,
+        tc.psum_pool(name="proj_psum", bufs=2) as proj_psum,
+        tc.psum_pool(name="score_psum", bufs=2) as score_psum,
+        tc.psum_pool(name="flip_psum", bufs=2) as flip_psum,
+        tc.psum_pool(name="out_psum", bufs=2) as out_psum,
+    ):
+        offsets = held.tile([P, N_SEQ * SEQ // 16], U16, name="offsets")
+        nc.sync.dma_start(offsets[:], offs)
+        table = [held.tile([P, VOCAB], F32, name=f"table{f}") for f in range(N_FBLK)]
+        pos = [held.tile([P, SEQ], F32, name=f"pos{f}") for f in range(N_FBLK)]
+        for f in range(N_FBLK):
+            nc.sync.dma_start(table[f][:], wtok[f * P : (f + 1) * P, :])
+            nc.scalar.dma_start(pos[f][:], wpos[f * P : (f + 1) * P, :])
+        weights = {}
+        for name, w in (("v", wv), ("q", wq), ("k", wk)):
+            weights[name] = held.tile([P, N_FBLK, FEATURES], BF16, name=f"w{name}")
+            nc.gpsimd.dma_start(weights[name][:], w.rearrange("(f p) m -> p f m", p=P))
+        bq_sb = held.tile([P, N_HEAD], F32, name="bq_sb")
+        nc.scalar.dma_start(bq_sb[:], bq.rearrange("(h p) o -> p (h o)", p=P))
+        bv_sb = held.tile([P, N_HEAD], F32, name="bv_sb")
+        nc.scalar.dma_start(bv_sb[:], bv.rearrange("(h p) o -> p (h o)", p=P))
+        bq_scaled = held.tile([P, N_HEAD], F32, name="bq_scaled")
+        nc.vector.tensor_scalar_mul(bq_scaled[:], bq_sb[:], SCALE)
+
+        identity = held.tile([P, P], BF16, name="identity")
+        make_identity(nc, identity[:])
+        causal = held.tile([P, P], BF16, name="causal")
+        nc.gpsimd.memset(causal[:], 0.0)
+        nc.gpsimd.affine_select(
+            out=causal[:], in_=causal[:], pattern=[[-1, P]], compare_op=IS_GE,
+            fill=MASKED, base=0, channel_multiplier=1,
+        )
+
+        for r in range(N_SEQ):
+            piece = offsets[:, r * (SEQ // 16) : (r + 1) * (SEQ // 16)]
+            x_bf = seqpool.tile([P, N_FBLK, SEQ], BF16, name="x_bf")
+            for f in range(N_FBLK):
+                x_f32 = xpool.tile([P, SEQ], F32, name="x_f32")
+                nc.vector.tensor_tensor(x_f32[:], table[f][:].indirect(piece), pos[f][:], ADD)
+                nc.vector.tensor_copy(x_bf[:, f, :], x_f32[:])
+
+            v_tok = seqpool.tile([P, N_TBLK, FEATURES], BF16, name="v_tok")
+            for t in range(N_TBLK):
+                v_ps = proj_psum.tile([P, FEATURES], F32, name="proj_ps")
+                for f in range(N_FBLK):
+                    nc.tensor.matmul(
+                        v_ps[:], x_bf[:, f, t * P : (t + 1) * P], weights["v"][:, f, :],
+                        start=(f == 0), stop=(f == N_FBLK - 1),
+                    )
+                nc.scalar.copy(v_tok[:, t, :], v_ps[:])
+
+            for h in range(N_HEAD):
+                head = slice(h * P, (h + 1) * P)
+                q_ps = proj_psum.tile([P, SEQ], F32, name="proj_ps")
+                for f in range(N_FBLK):
+                    nc.tensor.matmul(
+                        q_ps[:], weights["q"][:, f, head], x_bf[:, f, :],
+                        start=(f == 0), stop=(f == N_FBLK - 1),
+                    )
+                q_bf = headpool.tile([P, SEQ], BF16, name="q_bf")
+                nc.scalar.activation(q_bf[:], q_ps[:], IDENTITY, bias=bq_scaled[:, h : h + 1], scale=SCALE)
+                k_ps = proj_psum.tile([P, SEQ], F32, name="proj_ps")
+                for f in range(N_FBLK):
+                    nc.tensor.matmul(
+                        k_ps[:], weights["k"][:, f, head], x_bf[:, f, :],
+                        start=(f == 0), stop=(f == N_FBLK - 1),
+                    )
+                k_bf = headpool.tile([P, SEQ], BF16, name="k_bf")
+                nc.scalar.copy(k_bf[:], k_ps[:])
+
+                p_flip = headpool.tile([P, N_TBLK, SEQ], BF16, name="p_flip")
+                for b in range(N_TBLK):
+                    rows = slice(b * P, (b + 1) * P)
+                    width = (b + 1) * P
+                    score = score_psum.tile([P, SEQ], F32, name="score")
+                    nc.tensor.matmul(score[:, :width], q_bf[:, rows], k_bf[:, :width], start=True, stop=False)
+                    nc.tensor.matmul(score[:, rows], identity[:], causal[:], start=False, stop=True)
+                    neg_max = rowpool.tile([P, 1], F32, name="neg_max")
+                    nc.vector.tensor_reduce(neg_max[:], score[:, :width], axis=X_AXIS, op=MAX, negate=True)
+                    e_f32 = rowpool.tile([P, SEQ], F32, name="e_f32")
+                    e_sum = rowpool.tile([P, 1], F32, name="e_sum")
+                    nc.scalar.activation(
+                        e_f32[:, :width], score[:, :width], EXP, bias=neg_max[:], scale=1.0, accum_out=e_sum[:]
+                    )
+                    e_inv = rowpool.tile([P, 1], F32, name="e_inv")
+                    nc.vector.reciprocal(e_inv[:], e_sum[:])
+                    p_bf = rowpool.tile([P, SEQ], BF16, name="p_bf")
+                    nc.vector.tensor_scalar_mul(p_bf[:, :width], e_f32[:, :width], e_inv[:])
+                    flip = flip_psum.tile([P, N_TBLK, P], BF16, name="flip")
+                    for t in range(b + 1):
+                        nc.tensor.transpose(flip[:, t, :], p_bf[:, t * P : (t + 1) * P], identity[:])
+                    nc.vector.tensor_copy(p_flip[:, : b + 1, rows], flip[:, : b + 1, :])
+
+                o_ps = out_psum.tile([P, SEQ], F32, name="o_ps")
+                for t in range(N_TBLK):
+                    nc.tensor.matmul(
+                        o_ps[:, t * P :], v_tok[:, t, head], p_flip[:, t, t * P :],
+                        start=(t == 0), stop=(t == N_TBLK - 1),
+                    )
+                o_sb = headpool.tile([P, SEQ], F32, name="o_sb")
+                nc.scalar.activation(o_sb[:], o_ps[:], IDENTITY, bias=bv_sb[:, h : h + 1], scale=1.0)
+                nc.sync.dma_start(out[head, r * SEQ : (r + 1) * SEQ], o_sb[:])

@@ -32,13 +32,13 @@ def tile_thetransformer_b_kernel(tc, wtok, wpos, wq, bq, wk, wv, bv, offs, out):
     with (
         tc.tile_pool(name="held", bufs=1) as held,
         tc.tile_pool(name="xpool", bufs=4) as xpool,
-        tc.tile_pool(name="seqpool", bufs=2) as seqpool,
+        tc.tile_pool(name="seqpool", bufs=3) as seqpool,
         tc.tile_pool(name="headpool", bufs=3) as headpool,
         tc.tile_pool(name="rowpool", bufs=4) as rowpool,
         tc.psum_pool(name="proj_psum", bufs=2) as proj_psum,
-        tc.psum_pool(name="score_psum", bufs=2) as score_psum,
+        tc.psum_pool(name="score_psum", bufs=3) as score_psum,
         tc.psum_pool(name="flip_psum", bufs=2) as flip_psum,
-        tc.psum_pool(name="out_psum", bufs=2) as out_psum,
+        tc.psum_pool(name="out_psum", bufs=1) as out_psum,
     ):
         offsets = held.tile([P, N_SEQ * SEQ // 16], U16, name="offsets")
         nc.sync.dma_start(offsets[:], offs)
@@ -47,16 +47,16 @@ def tile_thetransformer_b_kernel(tc, wtok, wpos, wq, bq, wk, wv, bv, offs, out):
         for f in range(N_FBLK):
             nc.sync.dma_start(table[f][:], wtok[f * P : (f + 1) * P, :])
             nc.scalar.dma_start(pos[f][:], wpos[f * P : (f + 1) * P, :])
-        weights = {}
-        for name, w in (("v", wv), ("q", wq), ("k", wk)):
-            weights[name] = held.tile([P, N_FBLK, FEATURES], BF16, name=f"w{name}")
-            nc.gpsimd.dma_start(weights[name][:], w.rearrange("(f p) m -> p f m", p=P))
+        wv_sb = held.tile([P, N_FBLK, FEATURES], BF16, name="wv_sb")
+        nc.scalar.dma_start(wv_sb[:], wv.rearrange("(f p) m -> p f m", p=P))
+        wq_sb = held.tile([P, N_FBLK, FEATURES], BF16, name="wq_sb")
+        nc.scalar.dma_start(wq_sb[:], wq.rearrange("(f p) m -> p f m", p=P))
+        wk_sb = held.tile([P, N_FBLK, FEATURES], BF16, name="wk_sb")
+        nc.sync.dma_start(wk_sb[:], wk.rearrange("(f p) m -> p f m", p=P))
         bq_sb = held.tile([P, N_HEAD], F32, name="bq_sb")
         nc.scalar.dma_start(bq_sb[:], bq.rearrange("(h p) o -> p (h o)", p=P))
         bv_sb = held.tile([P, N_HEAD], F32, name="bv_sb")
         nc.scalar.dma_start(bv_sb[:], bv.rearrange("(h p) o -> p (h o)", p=P))
-        bq_scaled = held.tile([P, N_HEAD], F32, name="bq_scaled")
-        nc.vector.tensor_scalar_mul(bq_scaled[:], bq_sb[:], SCALE)
 
         identity = held.tile([P, P], BF16, name="identity")
         make_identity(nc, identity[:])
@@ -66,73 +66,118 @@ def tile_thetransformer_b_kernel(tc, wtok, wpos, wq, bq, wk, wv, bv, offs, out):
             out=causal[:], in_=causal[:], pattern=[[-1, P]], compare_op=IS_GE,
             fill=MASKED, base=0, channel_multiplier=1,
         )
+        bq_scaled = held.tile([P, N_HEAD], F32, name="bq_scaled")
+        nc.gpsimd.tensor_scalar_mul(bq_scaled[:], bq_sb[:], SCALE)
 
-        for r in range(N_SEQ):
+        x_bf, v_tok = {}, {}
+        q_bf, k_bf, p_rows, p_flip = {}, {}, {}, {}
+        e_f32, e_sum = {}, {}
+
+        def look_up(r, f):
+            if f == 0:
+                x_bf[r] = seqpool.tile([P, N_FBLK, SEQ], BF16, name="x_bf")
             piece = offsets[:, r * (SEQ // 16) : (r + 1) * (SEQ // 16)]
-            x_bf = seqpool.tile([P, N_FBLK, SEQ], BF16, name="x_bf")
+            x_f32 = xpool.tile([P, SEQ], F32, name="x_f32")
+            nc.vector.tensor_tensor(x_f32[:], table[f][:].indirect(piece), pos[f][:], ADD)
+            nc.vector.tensor_copy(x_bf[r][:, f, :], x_f32[:])
+
+        def project_v(r, t):
+            if t == 0:
+                v_tok[r] = seqpool.tile([P, N_TBLK, FEATURES], BF16, name="v_tok")
+            v_ps = proj_psum.tile([P, FEATURES], F32, name="proj_ps")
             for f in range(N_FBLK):
-                x_f32 = xpool.tile([P, SEQ], F32, name="x_f32")
-                nc.vector.tensor_tensor(x_f32[:], table[f][:].indirect(piece), pos[f][:], ADD)
-                nc.vector.tensor_copy(x_bf[:, f, :], x_f32[:])
+                nc.tensor.matmul(
+                    v_ps[:], x_bf[r][:, f, t * P : (t + 1) * P], wv_sb[:, f, :],
+                    start=(f == 0), stop=(f == N_FBLK - 1),
+                )
+            nc.scalar.copy(v_tok[r][:, t, :], v_ps[:])
 
-            v_tok = seqpool.tile([P, N_TBLK, FEATURES], BF16, name="v_tok")
+        def project_q(n):
+            r, h = divmod(n, N_HEAD)
+            q_ps = proj_psum.tile([P, SEQ], F32, name="proj_ps")
+            for f in range(N_FBLK):
+                nc.tensor.matmul(
+                    q_ps[:], wq_sb[:, f, h * P : (h + 1) * P], x_bf[r][:, f, :],
+                    start=(f == 0), stop=(f == N_FBLK - 1),
+                )
+            q_bf[n] = headpool.tile([P, SEQ], BF16, name="q_bf")
+            nc.scalar.activation(q_bf[n][:], q_ps[:], IDENTITY, bias=bq_scaled[:, h : h + 1], scale=SCALE)
+
+        def project_k(n):
+            r, h = divmod(n, N_HEAD)
+            k_ps = proj_psum.tile([P, SEQ], F32, name="proj_ps")
+            for f in range(N_FBLK):
+                nc.tensor.matmul(
+                    k_ps[:], wk_sb[:, f, h * P : (h + 1) * P], x_bf[r][:, f, :],
+                    start=(f == 0), stop=(f == N_FBLK - 1),
+                )
+            k_bf[n] = headpool.tile([P, SEQ], BF16, name="k_bf")
+            nc.scalar.copy(k_bf[n][:], k_ps[:])
+
+        def score_rows(n, b):
+            rows = slice(b * P, (b + 1) * P)
+            width = (b + 1) * P
+            score = score_psum.tile([P, SEQ], F32, name="score")
+            nc.tensor.matmul(score[:, :width], q_bf[n][:, rows], k_bf[n][:, :width], start=True, stop=False)
+            nc.tensor.matmul(score[:, rows], identity[:], causal[:], start=False, stop=True)
+            neg_max = rowpool.tile([P, 1], F32, name="neg_max")
+            nc.vector.tensor_reduce(neg_max[:], score[:, :width], axis=X_AXIS, op=MAX, negate=True)
+            e_f32[b] = rowpool.tile([P, SEQ], F32, name="e_f32")
+            e_sum[b] = rowpool.tile([P, 1], F32, name="e_sum")
+            nc.scalar.activation(
+                e_f32[b][:, :width], score[:, :width], EXP, bias=neg_max[:], scale=1.0, accum_out=e_sum[b][:]
+            )
+
+        def normalise_rows(n, b):
+            width = (b + 1) * P
+            e_inv = rowpool.tile([P, 1], F32, name="e_inv")
+            nc.vector.reciprocal(e_inv[:], e_sum[b][:])
+            nc.vector.tensor_scalar_mul(p_rows[n][:, b, :width], e_f32[b][:, :width], e_inv[:])
+
+        def flip_rows(n, b):
+            flip = flip_psum.tile([P, N_TBLK, P], BF16, name="flip")
+            for t in range(b + 1):
+                nc.tensor.transpose(flip[:, t, :], p_rows[n][:, b, t * P : (t + 1) * P], identity[:])
+            nc.vector.tensor_copy(p_flip[n][:, : b + 1, b * P : (b + 1) * P], flip[:, : b + 1, :])
+
+        def weigh_values(n):
+            r, h = divmod(n, N_HEAD)
+            head = slice(h * P, (h + 1) * P)
+            o_ps = out_psum.tile([P, SEQ], F32, name="o_ps")
             for t in range(N_TBLK):
-                v_ps = proj_psum.tile([P, FEATURES], F32, name="proj_ps")
-                for f in range(N_FBLK):
-                    nc.tensor.matmul(
-                        v_ps[:], x_bf[:, f, t * P : (t + 1) * P], weights["v"][:, f, :],
-                        start=(f == 0), stop=(f == N_FBLK - 1),
-                    )
-                nc.scalar.copy(v_tok[:, t, :], v_ps[:])
+                nc.tensor.matmul(
+                    o_ps[:, t * P :], v_tok[r][:, t, head], p_flip[n][:, t, t * P :],
+                    start=(t == 0), stop=(t == N_TBLK - 1),
+                )
+            o_sb = headpool.tile([P, SEQ], F32, name="o_sb")
+            nc.scalar.activation(o_sb[:], o_ps[:], IDENTITY, bias=bv_sb[:, h : h + 1], scale=1.0)
+            nc.sync.dma_start(out[head, r * SEQ : (r + 1) * SEQ], o_sb[:])
 
-            for h in range(N_HEAD):
-                head = slice(h * P, (h + 1) * P)
-                q_ps = proj_psum.tile([P, SEQ], F32, name="proj_ps")
-                for f in range(N_FBLK):
-                    nc.tensor.matmul(
-                        q_ps[:], weights["q"][:, f, head], x_bf[:, f, :],
-                        start=(f == 0), stop=(f == N_FBLK - 1),
-                    )
-                q_bf = headpool.tile([P, SEQ], BF16, name="q_bf")
-                nc.scalar.activation(q_bf[:], q_ps[:], IDENTITY, bias=bq_scaled[:, h : h + 1], scale=SCALE)
-                k_ps = proj_psum.tile([P, SEQ], F32, name="proj_ps")
-                for f in range(N_FBLK):
-                    nc.tensor.matmul(
-                        k_ps[:], weights["k"][:, f, head], x_bf[:, f, :],
-                        start=(f == 0), stop=(f == N_FBLK - 1),
-                    )
-                k_bf = headpool.tile([P, SEQ], BF16, name="k_bf")
-                nc.scalar.copy(k_bf[:], k_ps[:])
-
-                p_flip = headpool.tile([P, N_TBLK, SEQ], BF16, name="p_flip")
-                for b in range(N_TBLK):
-                    rows = slice(b * P, (b + 1) * P)
-                    width = (b + 1) * P
-                    score = score_psum.tile([P, SEQ], F32, name="score")
-                    nc.tensor.matmul(score[:, :width], q_bf[:, rows], k_bf[:, :width], start=True, stop=False)
-                    nc.tensor.matmul(score[:, rows], identity[:], causal[:], start=False, stop=True)
-                    neg_max = rowpool.tile([P, 1], F32, name="neg_max")
-                    nc.vector.tensor_reduce(neg_max[:], score[:, :width], axis=X_AXIS, op=MAX, negate=True)
-                    e_f32 = rowpool.tile([P, SEQ], F32, name="e_f32")
-                    e_sum = rowpool.tile([P, 1], F32, name="e_sum")
-                    nc.scalar.activation(
-                        e_f32[:, :width], score[:, :width], EXP, bias=neg_max[:], scale=1.0, accum_out=e_sum[:]
-                    )
-                    e_inv = rowpool.tile([P, 1], F32, name="e_inv")
-                    nc.vector.reciprocal(e_inv[:], e_sum[:])
-                    p_bf = rowpool.tile([P, SEQ], BF16, name="p_bf")
-                    nc.vector.tensor_scalar_mul(p_bf[:, :width], e_f32[:, :width], e_inv[:])
-                    flip = flip_psum.tile([P, N_TBLK, P], BF16, name="flip")
-                    for t in range(b + 1):
-                        nc.tensor.transpose(flip[:, t, :], p_bf[:, t * P : (t + 1) * P], identity[:])
-                    nc.vector.tensor_copy(p_flip[:, : b + 1, rows], flip[:, : b + 1, :])
-
-                o_ps = out_psum.tile([P, SEQ], F32, name="o_ps")
-                for t in range(N_TBLK):
-                    nc.tensor.matmul(
-                        o_ps[:, t * P :], v_tok[:, t, head], p_flip[:, t, t * P :],
-                        start=(t == 0), stop=(t == N_TBLK - 1),
-                    )
-                o_sb = headpool.tile([P, SEQ], F32, name="o_sb")
-                nc.scalar.activation(o_sb[:], o_ps[:], IDENTITY, bias=bv_sb[:, h : h + 1], scale=1.0)
-                nc.sync.dma_start(out[head, r * SEQ : (r + 1) * SEQ], o_sb[:])
+        n_task = N_SEQ * N_HEAD
+        for n in range(-8, n_task):
+            weighed = n >= 0
+            scored = 0 <= n + 1 < n_task
+            projected = 0 <= n + 2 < n_task
+            if scored:
+                p_rows[n + 1] = headpool.tile([P, N_TBLK, SEQ], BF16, name="p_rows")
+            if weighed:
+                p_flip[n] = headpool.tile([P, N_TBLK, SEQ], BF16, name="p_flip")
+            for b in (3, 2, 1, 0):
+                if b == 3 and projected:
+                    project_q(n + 2)
+                if b == 2 and projected:
+                    project_k(n + 2)
+                if b == 1 and 0 <= n + 4 < n_task:
+                    project_v((n + 4) // N_TBLK, (n + 4) % N_TBLK)
+                if weighed:
+                    flip_rows(n, b)
+                if scored:
+                    score_rows(n + 1, b)
+                    if b < 3:
+                        normalise_rows(n + 1, b + 1)
+            if scored:
+                normalise_rows(n + 1, 0)
+            if weighed:
+                weigh_values(n)
+            if n + 8 < n_task:
+                look_up((n + 8) // N_FBLK, (n + 8) % N_FBLK)

@@ -32,8 +32,8 @@ def tile_thetransformer_b_kernel(tc, wtok, wpos, wq, bq, wk, wv, bv, offs, out):
     with (
         tc.tile_pool(name="held", bufs=1) as held,
         tc.tile_pool(name="xpool", bufs=4) as xpool,
-        tc.tile_pool(name="seqpool", bufs=3) as seqpool,
-        tc.tile_pool(name="headpool", bufs=3) as headpool,
+        tc.tile_pool(name="seqpool", bufs=2) as seqpool,
+        tc.tile_pool(name="headpool", bufs=4) as headpool,
         tc.tile_pool(name="rowpool", bufs=4) as rowpool,
         tc.psum_pool(name="proj_psum", bufs=2) as proj_psum,
         tc.psum_pool(name="score_psum", bufs=3) as score_psum,
@@ -46,17 +46,17 @@ def tile_thetransformer_b_kernel(tc, wtok, wpos, wq, bq, wk, wv, bv, offs, out):
         pos = [held.tile([P, SEQ], F32, name=f"pos{f}") for f in range(N_FBLK)]
         for f in range(N_FBLK):
             nc.sync.dma_start(table[f][:], wtok[f * P : (f + 1) * P, :])
-            nc.scalar.dma_start(pos[f][:], wpos[f * P : (f + 1) * P, :])
-        wv_sb = held.tile([P, N_FBLK, FEATURES], BF16, name="wv_sb")
-        nc.scalar.dma_start(wv_sb[:], wv.rearrange("(f p) m -> p f m", p=P))
+            nc.sync.dma_start(pos[f][:], wpos[f * P : (f + 1) * P, :])
         wq_sb = held.tile([P, N_FBLK, FEATURES], BF16, name="wq_sb")
-        nc.scalar.dma_start(wq_sb[:], wq.rearrange("(f p) m -> p f m", p=P))
+        nc.sync.dma_start(wq_sb[:], wq.rearrange("(f p) m -> p f m", p=P))
         wk_sb = held.tile([P, N_FBLK, FEATURES], BF16, name="wk_sb")
         nc.sync.dma_start(wk_sb[:], wk.rearrange("(f p) m -> p f m", p=P))
+        wv_sb = held.tile([P, N_FBLK, FEATURES], BF16, name="wv_sb")
+        nc.sync.dma_start(wv_sb[:], wv.rearrange("(f p) m -> p f m", p=P))
         bq_sb = held.tile([P, N_HEAD], F32, name="bq_sb")
-        nc.scalar.dma_start(bq_sb[:], bq.rearrange("(h p) o -> p (h o)", p=P))
+        nc.gpsimd.dma_start(bq_sb[:], bq.rearrange("(h p) o -> p (h o)", p=P))
         bv_sb = held.tile([P, N_HEAD], F32, name="bv_sb")
-        nc.scalar.dma_start(bv_sb[:], bv.rearrange("(h p) o -> p (h o)", p=P))
+        nc.gpsimd.dma_start(bv_sb[:], bv.rearrange("(h p) o -> p (h o)", p=P))
 
         identity = held.tile([P, P], BF16, name="identity")
         make_identity(nc, identity[:])
@@ -154,22 +154,24 @@ def tile_thetransformer_b_kernel(tc, wtok, wpos, wq, bq, wk, wv, bv, offs, out):
             nc.sync.dma_start(out[head, r * SEQ : (r + 1) * SEQ], o_sb[:])
 
         n_task = N_SEQ * N_HEAD
-        for n in range(-8, n_task):
-            weighed = n >= 0
+        for n in range(-6, n_task + 2):
+            flipped = 0 <= n < n_task
             scored = 0 <= n + 1 < n_task
             projected = 0 <= n + 2 < n_task
             if scored:
                 p_rows[n + 1] = headpool.tile([P, N_TBLK, SEQ], BF16, name="p_rows")
-            if weighed:
+            if flipped:
                 p_flip[n] = headpool.tile([P, N_TBLK, SEQ], BF16, name="p_flip")
             for b in (3, 2, 1, 0):
                 if b == 3 and projected:
                     project_q(n + 2)
                 if b == 2 and projected:
                     project_k(n + 2)
-                if b == 1 and 0 <= n + 4 < n_task:
-                    project_v((n + 4) // N_TBLK, (n + 4) % N_TBLK)
-                if weighed:
+                if b == 1 and projected:
+                    project_v((n + 2) // N_HEAD, (n + 2) % N_HEAD)
+                if b == 0 and n >= 2:
+                    weigh_values(n - 2)
+                if flipped:
                     flip_rows(n, b)
                 if scored:
                     score_rows(n + 1, b)
@@ -177,7 +179,5 @@ def tile_thetransformer_b_kernel(tc, wtok, wpos, wq, bq, wk, wv, bv, offs, out):
                         normalise_rows(n + 1, b + 1)
             if scored:
                 normalise_rows(n + 1, 0)
-            if weighed:
-                weigh_values(n)
-            if n + 8 < n_task:
-                look_up((n + 8) // N_FBLK, (n + 8) % N_FBLK)
+            if n + 6 < n_task:
+                look_up((n + 6) // N_FBLK, (n + 6) % N_FBLK)

@@ -21,6 +21,7 @@ N_SEQ = 4
 N_HEAD = 4
 N_FBLK = FEATURES // P
 N_TBLK = SEQ // P
+N_PAIR = N_SEQ * N_HEAD // 2
 SCALE = 1.0 / math.sqrt(FEATURES)
 MASKED = -1.0e9
 
@@ -34,11 +35,11 @@ def tile_thetransformer_b_kernel(tc, wtok, wpos, wq, bq, wk, wv, bv, offs, out):
         tc.tile_pool(name="xpool", bufs=4) as xpool,
         tc.tile_pool(name="seqpool", bufs=2) as seqpool,
         tc.tile_pool(name="headpool", bufs=4) as headpool,
-        tc.tile_pool(name="rowpool", bufs=4) as rowpool,
-        tc.psum_pool(name="proj_psum", bufs=2) as proj_psum,
+        tc.tile_pool(name="pairpool", bufs=2) as pairpool,
+        tc.tile_pool(name="rowpool", bufs=6) as rowpool,
+        tc.psum_pool(name="wide_psum", bufs=3) as wide_psum,
         tc.psum_pool(name="score_psum", bufs=3) as score_psum,
         tc.psum_pool(name="flip_psum", bufs=2) as flip_psum,
-        tc.psum_pool(name="out_psum", bufs=1) as out_psum,
     ):
         offsets = held.tile([P, N_SEQ * SEQ // 16], U16, name="offsets")
         nc.sync.dma_start(offsets[:], offs)
@@ -60,6 +61,8 @@ def tile_thetransformer_b_kernel(tc, wtok, wpos, wq, bq, wk, wv, bv, offs, out):
 
         identity = held.tile([P, P], BF16, name="identity")
         make_identity(nc, identity[:])
+        identity_f32 = held.tile([P, P], F32, name="identity_f32")
+        make_identity(nc, identity_f32[:])
         causal = held.tile([P, P], BF16, name="causal")
         nc.gpsimd.memset(causal[:], 0.0)
         nc.gpsimd.affine_select(
@@ -70,7 +73,8 @@ def tile_thetransformer_b_kernel(tc, wtok, wpos, wq, bq, wk, wv, bv, offs, out):
         nc.gpsimd.tensor_scalar_mul(bq_scaled[:], bq_sb[:], SCALE)
 
         x_bf, v_tok = {}, {}
-        q_bf, k_bf, p_rows, p_flip = {}, {}, {}, {}
+        q_bf, k_bf = {}, {}
+        p_words, p_flip = {}, {}
         e_f32, e_sum = {}, {}
 
         def look_up(r, f):
@@ -84,7 +88,7 @@ def tile_thetransformer_b_kernel(tc, wtok, wpos, wq, bq, wk, wv, bv, offs, out):
         def project_v(r, t):
             if t == 0:
                 v_tok[r] = seqpool.tile([P, N_TBLK, FEATURES], BF16, name="v_tok")
-            v_ps = proj_psum.tile([P, FEATURES], F32, name="proj_ps")
+            v_ps = wide_psum.tile([P, FEATURES], F32, name="wide_ps")
             for f in range(N_FBLK):
                 nc.tensor.matmul(
                     v_ps[:], x_bf[r][:, f, t * P : (t + 1) * P], wv_sb[:, f, :],
@@ -94,7 +98,7 @@ def tile_thetransformer_b_kernel(tc, wtok, wpos, wq, bq, wk, wv, bv, offs, out):
 
         def project_q(n):
             r, h = divmod(n, N_HEAD)
-            q_ps = proj_psum.tile([P, SEQ], F32, name="proj_ps")
+            q_ps = wide_psum.tile([P, SEQ], F32, name="wide_ps")
             for f in range(N_FBLK):
                 nc.tensor.matmul(
                     q_ps[:], wq_sb[:, f, h * P : (h + 1) * P], x_bf[r][:, f, :],
@@ -105,7 +109,7 @@ def tile_thetransformer_b_kernel(tc, wtok, wpos, wq, bq, wk, wv, bv, offs, out):
 
         def project_k(n):
             r, h = divmod(n, N_HEAD)
-            k_ps = proj_psum.tile([P, SEQ], F32, name="proj_ps")
+            k_ps = wide_psum.tile([P, SEQ], F32, name="wide_ps")
             for f in range(N_FBLK):
                 nc.tensor.matmul(
                     k_ps[:], wk_sb[:, f, h * P : (h + 1) * P], x_bf[r][:, f, :],
@@ -122,62 +126,71 @@ def tile_thetransformer_b_kernel(tc, wtok, wpos, wq, bq, wk, wv, bv, offs, out):
             nc.tensor.matmul(score[:, rows], identity[:], causal[:], start=False, stop=True)
             neg_max = rowpool.tile([P, 1], F32, name="neg_max")
             nc.vector.tensor_reduce(neg_max[:], score[:, :width], axis=X_AXIS, op=MAX, negate=True)
-            e_f32[b] = rowpool.tile([P, SEQ], F32, name="e_f32")
-            e_sum[b] = rowpool.tile([P, 1], F32, name="e_sum")
+            e_f32[n, b] = rowpool.tile([P, SEQ], F32, name="e_f32")
+            e_sum[n, b] = rowpool.tile([P, 1], F32, name="e_sum")
             nc.scalar.activation(
-                e_f32[b][:, :width], score[:, :width], EXP, bias=neg_max[:], scale=1.0, accum_out=e_sum[b][:]
+                e_f32[n, b][:, :width], score[:, :width], EXP, bias=neg_max[:], scale=1.0, accum_out=e_sum[n, b][:]
             )
 
         def normalise_rows(n, b):
+            g, half = divmod(n, 2)
             width = (b + 1) * P
             e_inv = rowpool.tile([P, 1], F32, name="e_inv")
-            nc.vector.reciprocal(e_inv[:], e_sum[b][:])
-            nc.vector.tensor_scalar_mul(p_rows[n][:, b, :width], e_f32[b][:, :width], e_inv[:])
+            nc.vector.reciprocal(e_inv[:], e_sum[n, b][:])
+            halves = p_words[g][:, b, :width].bitcast(BF16)
+            nc.vector.tensor_scalar_mul(halves[:, half : 2 * width : 2], e_f32[n, b][:, :width], e_inv[:])
 
-        def flip_rows(n, b):
-            flip = flip_psum.tile([P, N_TBLK, P], BF16, name="flip")
+        def flip_rows(g, b):
+            flip = flip_psum.tile([P, N_TBLK, P], F32, name="flip")
             for t in range(b + 1):
-                nc.tensor.transpose(flip[:, t, :], p_rows[n][:, b, t * P : (t + 1) * P], identity[:])
-            nc.vector.tensor_copy(p_flip[n][:, : b + 1, b * P : (b + 1) * P], flip[:, : b + 1, :])
+                nc.tensor.transpose(flip[:, t, :], p_words[g][:, b, t * P : (t + 1) * P], identity_f32[:])
+            nc.vector.tensor_copy(p_flip[g][:, : b + 1, b * P : (b + 1) * P], flip[:, : b + 1, :])
 
         def weigh_values(n):
             r, h = divmod(n, N_HEAD)
+            g, half = divmod(n, 2)
             head = slice(h * P, (h + 1) * P)
-            o_ps = out_psum.tile([P, SEQ], F32, name="o_ps")
+            o_ps = wide_psum.tile([P, SEQ], F32, name="wide_ps")
             for t in range(N_TBLK):
+                halves = p_flip[g][:, t, t * P :].bitcast(BF16)
                 nc.tensor.matmul(
-                    o_ps[:, t * P :], v_tok[r][:, t, head], p_flip[n][:, t, t * P :],
+                    o_ps[:, t * P :], v_tok[r][:, t, head], halves[:, half :: 2],
                     start=(t == 0), stop=(t == N_TBLK - 1),
                 )
             o_sb = headpool.tile([P, SEQ], F32, name="o_sb")
             nc.scalar.activation(o_sb[:], o_ps[:], IDENTITY, bias=bv_sb[:, h : h + 1], scale=1.0)
             nc.sync.dma_start(out[head, r * SEQ : (r + 1) * SEQ], o_sb[:])
 
-        n_task = N_SEQ * N_HEAD
-        for n in range(-6, n_task + 2):
-            flipped = 0 <= n < n_task
-            scored = 0 <= n + 1 < n_task
-            projected = 0 <= n + 2 < n_task
+        for g in range(-4, N_PAIR + 2):
+            flipped = 0 <= g < N_PAIR
+            scored = 0 <= g + 1 < N_PAIR
+            projected = 0 <= g + 2 < N_PAIR
+            weighed = 0 <= g - 1 < N_PAIR
             if scored:
-                p_rows[n + 1] = headpool.tile([P, N_TBLK, SEQ], BF16, name="p_rows")
+                p_words[g + 1] = pairpool.tile([P, N_TBLK, SEQ], F32, name="p_words")
             if flipped:
-                p_flip[n] = headpool.tile([P, N_TBLK, SEQ], BF16, name="p_flip")
+                p_flip[g] = pairpool.tile([P, N_TBLK, SEQ], F32, name="p_flip")
             for b in (3, 2, 1, 0):
-                if b == 3 and projected:
-                    project_q(n + 2)
-                if b == 2 and projected:
-                    project_k(n + 2)
-                if b == 1 and projected:
-                    project_v((n + 2) // N_HEAD, (n + 2) % N_HEAD)
-                if b == 0 and n >= 2:
-                    weigh_values(n - 2)
-                if flipped:
-                    flip_rows(n, b)
-                if scored:
-                    score_rows(n + 1, b)
-                    if b < 3:
-                        normalise_rows(n + 1, b + 1)
+                for half in (0, 1):
+                    ahead = 2 * (g + 2) + half
+                    if b == 3 and projected:
+                        project_q(ahead)
+                    if b == 2 and projected:
+                        project_k(ahead)
+                    if b == 1 and scored:
+                        project_v((ahead - 2) // N_HEAD, (ahead - 2) % N_HEAD)
+                    if b == 0 and weighed:
+                        weigh_values(2 * (g - 1) + half)
+                    if half == 0 and flipped:
+                        flip_rows(g, b)
+                    if scored:
+                        score_rows(2 * (g + 1) + half, b)
+                        if b < 3:
+                            normalise_rows(2 * (g + 1) + half, b + 1)
             if scored:
-                normalise_rows(n + 1, 0)
-            if n + 6 < n_task:
-                look_up((n + 6) // N_FBLK, (n + 6) % N_FBLK)
+                normalise_rows(2 * (g + 1), 0)
+                normalise_rows(2 * (g + 1) + 1, 0)
+            for half in (0, 1):
+                later = 2 * (g + 4) + half
+                if later < N_SEQ * N_FBLK:
+                    look_up(later // N_FBLK, later % N_FBLK)

@@ -24,6 +24,7 @@ N_TBLK = SEQ // P
 N_PAIR = N_SEQ * N_HEAD // 2
 SCALE = 1.0 / math.sqrt(FEATURES)
 MASKED = -1.0e9
+WIDE_BANKS, SCORE_BANKS, FLIP_BANKS = 3, 3, 2
 
 FLOPS = 3 * 2 * FEATURES * FEATURES * N_SEQ * SEQ + 2 * 2 * P * (SEQ * (SEQ + 1) // 2) * N_HEAD * N_SEQ
 
@@ -37,22 +38,23 @@ def tile_thetransformer_b_kernel(tc, wtok, wpos, wq, bq, wk, wv, bv, offs, out):
         tc.tile_pool(name="headpool", bufs=4) as headpool,
         tc.tile_pool(name="pairpool", bufs=2) as pairpool,
         tc.tile_pool(name="rowpool", bufs=6) as rowpool,
-        tc.psum_pool(name="wide_psum", bufs=3) as wide_psum,
-        tc.psum_pool(name="score_psum", bufs=3) as score_psum,
-        tc.psum_pool(name="flip_psum", bufs=2) as flip_psum,
+        tc.psum_pool(name="wide_psum", bufs=WIDE_BANKS) as wide_psum,
+        tc.psum_pool(name="score_psum", bufs=SCORE_BANKS) as score_psum,
+        tc.psum_pool(name="flip_psum", bufs=FLIP_BANKS) as flip_psum,
     ):
         offsets = held.tile([P, N_SEQ * SEQ // 16], U16, name="offsets")
         nc.sync.dma_start(offsets[:], offs)
         table = [held.tile([P, VOCAB], F32, name=f"table{f}") for f in range(N_FBLK)]
         pos = [held.tile([P, SEQ], F32, name=f"pos{f}") for f in range(N_FBLK)]
-        for f in range(N_FBLK):
-            nc.sync.dma_start(table[f][:], wtok[f * P : (f + 1) * P, :])
-            nc.sync.dma_start(pos[f][:], wpos[f * P : (f + 1) * P, :])
         wq_sb = held.tile([P, N_FBLK, FEATURES], BF16, name="wq_sb")
-        nc.sync.dma_start(wq_sb[:], wq.rearrange("(f p) m -> p f m", p=P))
         wk_sb = held.tile([P, N_FBLK, FEATURES], BF16, name="wk_sb")
-        nc.sync.dma_start(wk_sb[:], wk.rearrange("(f p) m -> p f m", p=P))
         wv_sb = held.tile([P, N_FBLK, FEATURES], BF16, name="wv_sb")
+        for f in range(N_FBLK):
+            features = slice(f * P, (f + 1) * P)
+            nc.sync.dma_start(table[f][:], wtok[features, :])
+            nc.sync.dma_start(pos[f][:], wpos[features, :])
+            nc.sync.dma_start(wq_sb[:, f, :], wq[features, :])
+            nc.sync.dma_start(wk_sb[:, f, :], wk[features, :])
         nc.sync.dma_start(wv_sb[:], wv.rearrange("(f p) m -> p f m", p=P))
         bq_sb = held.tile([P, N_HEAD], F32, name="bq_sb")
         nc.gpsimd.dma_start(bq_sb[:], bq.rearrange("(h p) o -> p (h o)", p=P))
@@ -83,7 +85,7 @@ def tile_thetransformer_b_kernel(tc, wtok, wpos, wq, bq, wk, wv, bv, offs, out):
             piece = offsets[:, r * (SEQ // 16) : (r + 1) * (SEQ // 16)]
             x_f32 = xpool.tile([P, SEQ], F32, name="x_f32")
             nc.vector.tensor_tensor(x_f32[:], table[f][:].indirect(piece), pos[f][:], ADD)
-            nc.vector.tensor_copy(x_bf[r][:, f, :], x_f32[:])
+            nc.scalar.copy(x_bf[r][:, f, :], x_f32[:])
 
         def project_v(r, t):
             if t == 0:
@@ -96,27 +98,33 @@ def tile_thetransformer_b_kernel(tc, wtok, wpos, wq, bq, wk, wv, bv, offs, out):
                 )
             nc.scalar.copy(v_tok[r][:, t, :], v_ps[:])
 
-        def project_q(n):
+        def add_to_projection(sum_ps, w_sb, n, f):
             r, h = divmod(n, N_HEAD)
-            q_ps = wide_psum.tile([P, SEQ], F32, name="wide_ps")
-            for f in range(N_FBLK):
-                nc.tensor.matmul(
-                    q_ps[:], wq_sb[:, f, h * P : (h + 1) * P], x_bf[r][:, f, :],
-                    start=(f == 0), stop=(f == N_FBLK - 1),
-                )
+            nc.tensor.matmul(
+                sum_ps[:], w_sb[:, f, h * P : (h + 1) * P], x_bf[r][:, f, :],
+                start=(f == 0), stop=(f == N_FBLK - 1),
+            )
+
+        def keep_q(q_ps, n):
+            h = n % N_HEAD
             q_bf[n] = headpool.tile([P, SEQ], BF16, name="q_bf")
             nc.scalar.activation(q_bf[n][:], q_ps[:], IDENTITY, bias=bq_scaled[:, h : h + 1], scale=SCALE)
 
+        def keep_k(k_ps, n, copy):
+            k_bf[n] = headpool.tile([P, SEQ], BF16, name="k_bf")
+            copy(k_bf[n][:], k_ps[:])
+
+        def project_q(n):
+            q_ps = wide_psum.tile([P, SEQ], F32, name="wide_ps")
+            for f in range(N_FBLK):
+                add_to_projection(q_ps, wq_sb, n, f)
+            keep_q(q_ps, n)
+
         def project_k(n):
-            r, h = divmod(n, N_HEAD)
             k_ps = wide_psum.tile([P, SEQ], F32, name="wide_ps")
             for f in range(N_FBLK):
-                nc.tensor.matmul(
-                    k_ps[:], wk_sb[:, f, h * P : (h + 1) * P], x_bf[r][:, f, :],
-                    start=(f == 0), stop=(f == N_FBLK - 1),
-                )
-            k_bf[n] = headpool.tile([P, SEQ], BF16, name="k_bf")
-            nc.scalar.copy(k_bf[n][:], k_ps[:])
+                add_to_projection(k_ps, wk_sb, n, f)
+            keep_k(k_ps, n, nc.scalar.copy)
 
         def score_rows(n, b):
             rows = slice(b * P, (b + 1) * P)
@@ -161,10 +169,25 @@ def tile_thetransformer_b_kernel(tc, wtok, wpos, wq, bq, wk, wv, bv, offs, out):
             nc.scalar.activation(o_sb[:], o_ps[:], IDENTITY, bias=bv_sb[:, h : h + 1], scale=1.0)
             nc.sync.dma_start(out[head, r * SEQ : (r + 1) * SEQ], o_sb[:])
 
-        for g in range(-4, N_PAIR + 2):
+        banks = (
+            [score_psum.tile([P, SEQ], F32, name="score") for bank in range(SCORE_BANKS)]
+            + [flip_psum.tile([P, SEQ], F32, name="flip") for bank in range(FLIP_BANKS)]
+            + [wide_psum.tile([P, SEQ], F32, name="wide_ps") for bank in range(WIDE_BANKS)]
+        )
+        for f in range(N_FBLK):
+            look_up(0, f)
+            look_up(1, f)
+            for n in range(N_HEAD):
+                add_to_projection(banks[2 * n], wq_sb, n, f)
+                add_to_projection(banks[2 * n + 1], wk_sb, n, f)
+        for n in range(N_HEAD):
+            keep_q(banks[2 * n], n)
+            keep_k(banks[2 * n + 1], n, nc.vector.tensor_copy)
+
+        for g in range(-1, N_PAIR + 2):
             flipped = 0 <= g < N_PAIR
             scored = 0 <= g + 1 < N_PAIR
-            projected = 0 <= g + 2 < N_PAIR
+            projected = N_HEAD // 2 <= g + 2 < N_PAIR
             weighed = 0 <= g - 1 < N_PAIR
             if scored:
                 p_words[g + 1] = pairpool.tile([P, N_TBLK, SEQ], F32, name="p_words")
@@ -192,5 +215,5 @@ def tile_thetransformer_b_kernel(tc, wtok, wpos, wq, bq, wk, wv, bv, offs, out):
                 normalise_rows(2 * (g + 1) + 1, 0)
             for half in (0, 1):
                 later = 2 * (g + 4) + half
-                if later < N_SEQ * N_FBLK:
+                if 2 * N_FBLK <= later < N_SEQ * N_FBLK:
                     look_up(later // N_FBLK, later % N_FBLK)

@@ -8,6 +8,7 @@ BF16 = mybir.dt.bfloat16
 U16 = mybir.dt.uint16
 ADD = mybir.AluOpType.add
 MAX = mybir.AluOpType.max
+MULT = mybir.AluOpType.mult
 IS_GE = mybir.AluOpType.is_ge
 EXP = mybir.ActivationFunctionType.Exp
 IDENTITY = mybir.ActivationFunctionType.Identity
@@ -146,7 +147,9 @@ def tile_thetransformer_b_kernel(tc, wtok, wpos, wq, bq, wk, wv, bv, offs, out):
             e_inv = rowpool.tile([P, 1], F32, name="e_inv")
             nc.vector.reciprocal(e_inv[:], e_sum[n, b][:])
             halves = p_words[g][:, b, :width].bitcast(BF16)
-            nc.vector.tensor_scalar_mul(halves[:, half : 2 * width : 2], e_f32[n, b][:, :width], e_inv[:])
+            nc.gpsimd.tensor_scalar(
+                halves[:, half : 2 * width : 2], e_f32[n, b][:, :width], e_inv[:], 0.0, op0=MULT, op1=ADD
+            )
 
         def flip_rows(g, b):
             flip = flip_psum.tile([P, N_TBLK, P], F32, name="flip")

@@ -18,6 +18,7 @@ P = 128
 FEATURES = 512
 VOCAB = 1024
 SEQ = 512
+PIECE = SEQ // 2
 N_SEQ = 4
 N_HEAD = 4
 N_FBLK = FEATURES // P
@@ -35,6 +36,7 @@ def tile_thetransformer_b_kernel(tc, wtok, wpos, wq, bq, wk, wv, bv, offs, out):
     with (
         tc.tile_pool(name="held", bufs=1) as held,
         tc.tile_pool(name="xpool", bufs=4) as xpool,
+        tc.tile_pool(name="wholepool", bufs=3) as wholepool,
         tc.tile_pool(name="seqpool", bufs=2) as seqpool,
         tc.tile_pool(name="headpool", bufs=4) as headpool,
         tc.tile_pool(name="pairpool", bufs=2) as pairpool,
@@ -80,13 +82,14 @@ def tile_thetransformer_b_kernel(tc, wtok, wpos, wq, bq, wk, wv, bv, offs, out):
         p_words, p_flip = {}, {}
         e_f32, e_sum = {}, {}
 
-        def look_up(r, f):
-            if f == 0:
-                x_bf[r] = seqpool.tile([P, N_FBLK, SEQ], BF16, name="x_bf")
-            piece = offsets[:, r * (SEQ // 16) : (r + 1) * (SEQ // 16)]
-            x_f32 = xpool.tile([P, SEQ], F32, name="x_f32")
-            nc.vector.tensor_tensor(x_f32[:], table[f][:].indirect(piece), pos[f][:], ADD)
-            nc.scalar.copy(x_bf[r][:, f, :], x_f32[:])
+        def look_up(r, f, part):
+            if f == 0 and part == 0:
+                x_bf[r] = wholepool.tile([P, N_FBLK, SEQ], BF16, name="x_bf")
+            tokens = slice(part * PIECE, (part + 1) * PIECE)
+            piece = offsets[:, (r * SEQ + part * PIECE) // 16 : (r * SEQ + (part + 1) * PIECE) // 16]
+            x_f32 = xpool.tile([P, PIECE], F32, name="x_f32")
+            nc.vector.tensor_tensor(x_f32[:], table[f][:].indirect(piece), pos[f][:, tokens], ADD)
+            nc.scalar.copy(x_bf[r][:, f, tokens], x_f32[:])
 
         def project_v(r, t):
             if t == 0:
@@ -178,8 +181,9 @@ def tile_thetransformer_b_kernel(tc, wtok, wpos, wq, bq, wk, wv, bv, offs, out):
             + [wide_psum.tile([P, SEQ], F32, name="wide_ps") for bank in range(WIDE_BANKS)]
         )
         for f in range(N_FBLK):
-            look_up(0, f)
-            look_up(1, f)
+            for r in (0, 1):
+                look_up(r, f, 0)
+                look_up(r, f, 1)
             for n in range(N_HEAD):
                 add_to_projection(banks[2 * n], wq_sb, n, f)
                 add_to_projection(banks[2 * n + 1], wk_sb, n, f)
@@ -213,10 +217,9 @@ def tile_thetransformer_b_kernel(tc, wtok, wpos, wq, bq, wk, wv, bv, offs, out):
                         score_rows(2 * (g + 1) + half, b)
                         if b < 3:
                             normalise_rows(2 * (g + 1) + half, b + 1)
+                later = 2 * (g + 4) + (N_TBLK - 1 - b) // 2
+                if 2 * N_FBLK <= later < N_SEQ * N_FBLK:
+                    look_up(later // N_FBLK, later % N_FBLK, (N_TBLK - 1 - b) % 2)
             if scored:
                 normalise_rows(2 * (g + 1), 0)
                 normalise_rows(2 * (g + 1) + 1, 0)
-            for half in (0, 1):
-                later = 2 * (g + 4) + half
-                if 2 * N_FBLK <= later < N_SEQ * N_FBLK:
-                    look_up(later // N_FBLK, later % N_FBLK)

@@ -39,8 +39,8 @@ def tile_thetransformer_b_kernel(tc, wtok, wpos, wq, bq, wk, wv, bv, offs, out):
         tc.tile_pool(name="wholepool", bufs=3) as wholepool,
         tc.tile_pool(name="seqpool", bufs=2) as seqpool,
         tc.tile_pool(name="headpool", bufs=4) as headpool,
-        tc.tile_pool(name="pairpool", bufs=2) as pairpool,
-        tc.tile_pool(name="rowpool", bufs=6) as rowpool,
+        tc.tile_pool(name="pairpool", bufs=3) as pairpool,
+        tc.tile_pool(name="rowpool", bufs=10) as rowpool,
         tc.psum_pool(name="wide_psum", bufs=WIDE_BANKS) as wide_psum,
         tc.psum_pool(name="score_psum", bufs=SCORE_BANKS) as score_psum,
         tc.psum_pool(name="flip_psum", bufs=FLIP_BANKS) as flip_psum,

@@ -80,7 +80,8 @@ def tile_thetransformer_b_kernel(tc, wtok, wpos, wq, bq, wk, wv, bv, offs, out):
         x_bf, v_tok = {}, {}
         q_bf, k_bf = {}, {}
         p_words, p_flip = {}, {}
-        e_f32, e_sum = {}, {}
+        e_f32 = {}
+        e_sum, e_inv = {}, {}
 
         def look_up(r, f, part):
             if f == 0 and part == 0:
@@ -139,19 +140,24 @@ def tile_thetransformer_b_kernel(tc, wtok, wpos, wq, bq, wk, wv, bv, offs, out):
             neg_max = rowpool.tile([P, 1], F32, name="neg_max")
             nc.vector.tensor_reduce(neg_max[:], score[:, :width], axis=X_AXIS, op=MAX, negate=True)
             e_f32[n, b] = rowpool.tile([P, SEQ], F32, name="e_f32")
-            e_sum[n, b] = rowpool.tile([P, 1], F32, name="e_sum")
+            g, half = divmod(n, 2)
+            if half == 0:
+                e_sum[g, b] = rowpool.tile([P, 2], F32, name="e_sum")
             nc.scalar.activation(
-                e_f32[n, b][:, :width], score[:, :width], EXP, bias=neg_max[:], scale=1.0, accum_out=e_sum[n, b][:]
+                e_f32[n, b][:, :width], score[:, :width], EXP, bias=neg_max[:], scale=1.0,
+                accum_out=e_sum[g, b][:, half : half + 1],
             )
 
         def normalise_rows(n, b):
             g, half = divmod(n, 2)
             width = (b + 1) * P
-            e_inv = rowpool.tile([P, 1], F32, name="e_inv")
-            nc.vector.reciprocal(e_inv[:], e_sum[n, b][:])
+            if half == 0:
+                e_inv[g, b] = rowpool.tile([P, 2], F32, name="e_inv")
+                nc.vector.reciprocal(e_inv[g, b][:], e_sum[g, b][:])
             halves = p_words[g][:, b, :width].bitcast(BF16)
             nc.gpsimd.tensor_scalar(
-                halves[:, half : 2 * width : 2], e_f32[n, b][:, :width], e_inv[:], 0.0, op0=MULT, op1=ADD
+                halves[:, half : 2 * width : 2], e_f32[n, b][:, :width], e_inv[g, b][:, half : half + 1], 0.0,
+                op0=MULT, op1=ADD,
             )
 
         def flip_rows(g, b):

@@ -39,6 +39,7 @@ def tile_thetransformer_b_kernel(tc, wtok, wpos, wq, bq, wk, wv, bv, offs, out):
         tc.tile_pool(name="wholepool", bufs=3) as wholepool,
         tc.tile_pool(name="seqpool", bufs=2) as seqpool,
         tc.tile_pool(name="headpool", bufs=4) as headpool,
+        tc.tile_pool(name="outpool", bufs=6) as outpool,
         tc.tile_pool(name="pairpool", bufs=3) as pairpool,
         tc.tile_pool(name="rowpool", bufs=10) as rowpool,
         tc.psum_pool(name="wide_psum", bufs=WIDE_BANKS) as wide_psum,
@@ -166,20 +167,25 @@ def tile_thetransformer_b_kernel(tc, wtok, wpos, wq, bq, wk, wv, bv, offs, out):
                 nc.tensor.transpose(flip[:, t, :], p_words[g][:, b, t * P : (t + 1) * P], identity_f32[:])
             nc.vector.tensor_copy(p_flip[g][:, : b + 1, b * P : (b + 1) * P], flip[:, : b + 1, :])
 
-        def weigh_values(n):
+        def weigh_values(n, first, behind, by_vector=False):
             r, h = divmod(n, N_HEAD)
             g, half = divmod(n, 2)
             head = slice(h * P, (h + 1) * P)
             o_ps = wide_psum.tile([P, SEQ], F32, name="wide_ps")
-            for t in range(N_TBLK):
-                halves = p_flip[g][:, t, t * P :].bitcast(BF16)
+            for t in range(behind):
+                columns = slice(max(t, first) * P, behind * P)
+                halves = p_flip[g][:, t, columns].bitcast(BF16)
                 nc.tensor.matmul(
-                    o_ps[:, t * P :], v_tok[r][:, t, head], halves[:, half :: 2],
-                    start=(t == 0), stop=(t == N_TBLK - 1),
+                    o_ps[:, columns], v_tok[r][:, t, head], halves[:, half :: 2],
+                    start=(t == 0), stop=(t == behind - 1),
                 )
-            o_sb = headpool.tile([P, SEQ], F32, name="o_sb")
-            nc.scalar.activation(o_sb[:], o_ps[:], IDENTITY, bias=bv_sb[:, h : h + 1], scale=1.0)
-            nc.sync.dma_start(out[head, r * SEQ : (r + 1) * SEQ], o_sb[:])
+            columns = slice(first * P, behind * P)
+            o_sb = outpool.tile([P, SEQ], F32, name="o_sb")
+            if by_vector:
+                nc.vector.tensor_scalar_add(o_sb[:, columns], o_ps[:, columns], bv_sb[:, h : h + 1])
+            else:
+                nc.scalar.activation(o_sb[:, columns], o_ps[:, columns], IDENTITY, bias=bv_sb[:, h : h + 1], scale=1.0)
+            nc.sync.dma_start(out[head, r * SEQ + first * P : r * SEQ + behind * P], o_sb[:, columns])
 
         banks = (
             [score_psum.tile([P, SEQ], F32, name="score") for bank in range(SCORE_BANKS)]
@@ -197,13 +203,12 @@ def tile_thetransformer_b_kernel(tc, wtok, wpos, wq, bq, wk, wv, bv, offs, out):
             keep_q(banks[2 * n], n)
             keep_k(banks[2 * n + 1], n, nc.vector.tensor_copy)
 
-        for g in range(-1, N_PAIR + 2):
-            flipped = 0 <= g < N_PAIR
-            scored = 0 <= g + 1 < N_PAIR
+        last = N_PAIR - 1
+        for g in range(-1, last):
+            flipped = 0 <= g
             projected = N_HEAD // 2 <= g + 2 < N_PAIR
-            weighed = 0 <= g - 1 < N_PAIR
-            if scored:
-                p_words[g + 1] = pairpool.tile([P, N_TBLK, SEQ], F32, name="p_words")
+            weighed = 0 <= g - 1
+            p_words[g + 1] = pairpool.tile([P, N_TBLK, SEQ], F32, name="p_words")
             if flipped:
                 p_flip[g] = pairpool.tile([P, N_TBLK, SEQ], F32, name="p_flip")
             for b in (3, 2, 1, 0):
@@ -213,19 +218,28 @@ def tile_thetransformer_b_kernel(tc, wtok, wpos, wq, bq, wk, wv, bv, offs, out):
                         project_q(ahead)
                     if b == 2 and projected:
                         project_k(ahead)
-                    if b == 1 and scored:
+                    if b == 1:
                         project_v((ahead - 2) // N_HEAD, (ahead - 2) % N_HEAD)
                     if b == 0 and weighed:
-                        weigh_values(2 * (g - 1) + half)
+                        weigh_values(2 * (g - 1) + half, 0, N_TBLK)
                     if half == 0 and flipped:
                         flip_rows(g, b)
-                    if scored:
-                        score_rows(2 * (g + 1) + half, b)
-                        if b < 3:
-                            normalise_rows(2 * (g + 1) + half, b + 1)
+                    score_rows(2 * (g + 1) + half, b)
+                    if b < 3:
+                        normalise_rows(2 * (g + 1) + half, b + 1)
                 later = 2 * (g + 4) + (N_TBLK - 1 - b) // 2
                 if 2 * N_FBLK <= later < N_SEQ * N_FBLK:
                     look_up(later // N_FBLK, later % N_FBLK, (N_TBLK - 1 - b) % 2)
-            if scored:
-                normalise_rows(2 * (g + 1), 0)
-                normalise_rows(2 * (g + 1) + 1, 0)
+            normalise_rows(2 * (g + 1), 0)
+            normalise_rows(2 * (g + 1) + 1, 0)
+
+        p_flip[last] = pairpool.tile([P, N_TBLK, SEQ], F32, name="p_flip")
+        for b in (3, 2, 1):
+            flip_rows(last, b)
+        for half in (0, 1):
+            weigh_values(2 * (last - 1) + half, 0, N_TBLK)
+        weigh_values(2 * last, 1, N_TBLK)
+        flip_rows(last, 0)
+        weigh_values(2 * last + 1, 1, N_TBLK, by_vector=True)
+        weigh_values(2 * last, 0, 1)
+        weigh_values(2 * last + 1, 0, 1, by_vector=True)

@@ -38,7 +38,7 @@ def tile_thetransformer_b_kernel(tc, wtok, wpos, wq, bq, wk, wv, bv, offs, out):
         tc.tile_pool(name="xpool", bufs=4) as xpool,
         tc.tile_pool(name="wholepool", bufs=3) as wholepool,
         tc.tile_pool(name="seqpool", bufs=2) as seqpool,
-        tc.tile_pool(name="headpool", bufs=4) as headpool,
+        tc.tile_pool(name="headpool", bufs=6) as headpool,
         tc.tile_pool(name="outpool", bufs=6) as outpool,
         tc.tile_pool(name="pairpool", bufs=3) as pairpool,
         tc.tile_pool(name="rowpool", bufs=10) as rowpool,
@@ -206,7 +206,6 @@ def tile_thetransformer_b_kernel(tc, wtok, wpos, wq, bq, wk, wv, bv, offs, out):
         last = N_PAIR - 1
         for g in range(-1, last):
             flipped = 0 <= g
-            projected = N_HEAD // 2 <= g + 2 < N_PAIR
             weighed = 0 <= g - 1
             p_words[g + 1] = pairpool.tile([P, N_TBLK, SEQ], F32, name="p_words")
             if flipped:
@@ -214,10 +213,10 @@ def tile_thetransformer_b_kernel(tc, wtok, wpos, wq, bq, wk, wv, bv, offs, out):
             for b in (3, 2, 1, 0):
                 for half in (0, 1):
                     ahead = 2 * (g + 2) + half
-                    if b == 3 and projected:
-                        project_q(ahead)
-                    if b == 2 and projected:
+                    if b == 3 and N_HEAD // 2 <= g + 2 < N_PAIR:
                         project_k(ahead)
+                    if b == 2 and N_HEAD // 2 <= g + 3 < N_PAIR:
+                        project_q(ahead + 2)
                     if b == 1:
                         project_v((ahead - 2) // N_HEAD, (ahead - 2) % N_HEAD)
                     if b == 0 and weighed:
@@ -227,7 +226,7 @@ def tile_thetransformer_b_kernel(tc, wtok, wpos, wq, bq, wk, wv, bv, offs, out):
                     score_rows(2 * (g + 1) + half, b)
                     if b < 3:
                         normalise_rows(2 * (g + 1) + half, b + 1)
-                later = 2 * (g + 4) + (N_TBLK - 1 - b) // 2
+                later = 2 * (g + 5) + (N_TBLK - 1 - b) // 2
                 if 2 * N_FBLK <= later < N_SEQ * N_FBLK:
                     look_up(later // N_FBLK, later % N_FBLK, (N_TBLK - 1 - b) % 2)
             normalise_rows(2 * (g + 1), 0)

@@ -213,9 +213,9 @@ def tile_thetransformer_b_kernel(tc, wtok, wpos, wq, bq, wk, wv, bv, offs, out):
             for b in (3, 2, 1, 0):
                 for half in (0, 1):
                     ahead = 2 * (g + 2) + half
-                    if b == 3 and N_HEAD // 2 <= g + 2 < N_PAIR:
-                        project_k(ahead)
-                    if b == 2 and N_HEAD // 2 <= g + 3 < N_PAIR:
+                    if b == (3 if g >= 0 else 0) and g + 3 < N_PAIR:
+                        project_k(ahead + 2)
+                    if b == 2 and g + 3 < N_PAIR:
                         project_q(ahead + 2)
                     if b == 1:
                         project_v((ahead - 2) // N_HEAD, (ahead - 2) % N_HEAD)

@@ -213,8 +213,10 @@ def tile_thetransformer_b_kernel(tc, wtok, wpos, wq, bq, wk, wv, bv, offs, out):
             for b in (3, 2, 1, 0):
                 for half in (0, 1):
                     ahead = 2 * (g + 2) + half
-                    if b == (3 if g >= 0 else 0) and g + 3 < N_PAIR:
+                    if b == (3 if g >= 0 else 0) and g + 3 < N_PAIR - 2:
                         project_k(ahead + 2)
+                    if b == 3 and N_PAIR - 2 <= g + 2 < N_PAIR:
+                        project_k(ahead)
                     if b == 2 and g + 3 < N_PAIR:
                         project_q(ahead + 2)
                     if b == 1:

import math

import concourse.mybir as mybir
from concourse.masks import make_identity

F32 = mybir.dt.float32
BF16 = mybir.dt.bfloat16
U16 = mybir.dt.uint16
ADD = mybir.AluOpType.add
MAX = mybir.AluOpType.max
MULT = mybir.AluOpType.mult
IS_GE = mybir.AluOpType.is_ge
EXP = mybir.ActivationFunctionType.Exp
IDENTITY = mybir.ActivationFunctionType.Identity
X_AXIS = mybir.AxisListType.X

P = 128
FEATURES = 512
VOCAB = 1024
SEQ = 512
PIECE = SEQ // 2
N_SEQ = 4
N_HEAD = 4
N_FBLK = FEATURES // P
N_TBLK = SEQ // P
N_PAIR = N_SEQ * N_HEAD // 2
SCALE = 1.0 / math.sqrt(FEATURES)
MASKED = -1.0e9
WIDE_BANKS, SCORE_BANKS, FLIP_BANKS = 3, 3, 2

FLOPS = 3 * 2 * FEATURES * FEATURES * N_SEQ * SEQ + 2 * 2 * P * (SEQ * (SEQ + 1) // 2) * N_HEAD * N_SEQ


def tile_thetransformer_b_kernel(tc, wtok, wpos, wq, bq, wk, wv, bv, offs, out):
    nc = tc.nc
    with (
        tc.tile_pool(name="held", bufs=1) as held,
        tc.tile_pool(name="xpool", bufs=4) as xpool,
        tc.tile_pool(name="wholepool", bufs=3) as wholepool,
        tc.tile_pool(name="seqpool", bufs=2) as seqpool,
        tc.tile_pool(name="headpool", bufs=6) as headpool,
        tc.tile_pool(name="outpool", bufs=6) as outpool,
        tc.tile_pool(name="pairpool", bufs=3) as pairpool,
        tc.tile_pool(name="rowpool", bufs=10) as rowpool,
        tc.psum_pool(name="wide_psum", bufs=WIDE_BANKS) as wide_psum,
        tc.psum_pool(name="score_psum", bufs=SCORE_BANKS) as score_psum,
        tc.psum_pool(name="flip_psum", bufs=FLIP_BANKS) as flip_psum,
    ):
        offsets = held.tile([P, N_SEQ * SEQ // 16], U16, name="offsets")
        nc.sync.dma_start(offsets[:], offs)
        table = [held.tile([P, VOCAB], F32, name=f"table{f}") for f in range(N_FBLK)]
        pos = [held.tile([P, SEQ], F32, name=f"pos{f}") for f in range(N_FBLK)]
        wq_sb = held.tile([P, N_FBLK, FEATURES], BF16, name="wq_sb")
        wk_sb = held.tile([P, N_FBLK, FEATURES], BF16, name="wk_sb")
        wv_sb = held.tile([P, N_FBLK, FEATURES], BF16, name="wv_sb")
        for f in range(N_FBLK):
            features = slice(f * P, (f + 1) * P)
            nc.sync.dma_start(table[f][:], wtok[features, :])
            nc.sync.dma_start(pos[f][:], wpos[features, :])
            nc.sync.dma_start(wq_sb[:, f, :], wq[features, :])
            nc.sync.dma_start(wk_sb[:, f, :], wk[features, :])
        nc.sync.dma_start(wv_sb[:], wv.rearrange("(f p) m -> p f m", p=P))
        bq_sb = held.tile([P, N_HEAD], F32, name="bq_sb")
        nc.gpsimd.dma_start(bq_sb[:], bq.rearrange("(h p) o -> p (h o)", p=P))
        bv_sb = held.tile([P, N_HEAD], F32, name="bv_sb")
        nc.gpsimd.dma_start(bv_sb[:], bv.rearrange("(h p) o -> p (h o)", p=P))

        identity = held.tile([P, P], BF16, name="identity")
        make_identity(nc, identity[:])
        identity_f32 = held.tile([P, P], F32, name="identity_f32")
        make_identity(nc, identity_f32[:])
        causal = held.tile([P, P], BF16, name="causal")
        nc.gpsimd.memset(causal[:], 0.0)
        nc.gpsimd.affine_select(
            out=causal[:], in_=causal[:], pattern=[[-1, P]], compare_op=IS_GE,
            fill=MASKED, base=0, channel_multiplier=1,
        )
        bq_scaled = held.tile([P, N_HEAD], F32, name="bq_scaled")
        nc.gpsimd.tensor_scalar_mul(bq_scaled[:], bq_sb[:], SCALE)

        x_bf, v_tok = {}, {}
        q_bf, k_bf = {}, {}
        p_words, p_flip = {}, {}
        e_f32 = {}
        e_sum, e_inv = {}, {}

        def look_up(r, f, part):
            if f == 0 and part == 0:
                x_bf[r] = wholepool.tile([P, N_FBLK, SEQ], BF16, name="x_bf")
            tokens = slice(part * PIECE, (part + 1) * PIECE)
            piece = offsets[:, (r * SEQ + part * PIECE) // 16 : (r * SEQ + (part + 1) * PIECE) // 16]
            x_f32 = xpool.tile([P, PIECE], F32, name="x_f32")
            nc.vector.tensor_tensor(x_f32[:], table[f][:].indirect(piece), pos[f][:, tokens], ADD)
            nc.scalar.copy(x_bf[r][:, f, tokens], x_f32[:])

        def project_v(r, t):
            if t == 0:
                v_tok[r] = seqpool.tile([P, N_TBLK, FEATURES], BF16, name="v_tok")
            v_ps = wide_psum.tile([P, FEATURES], F32, name="wide_ps")
            for f in range(N_FBLK):
                nc.tensor.matmul(
                    v_ps[:], x_bf[r][:, f, t * P : (t + 1) * P], wv_sb[:, f, :],
                    start=(f == 0), stop=(f == N_FBLK - 1),
                )
            nc.scalar.copy(v_tok[r][:, t, :], v_ps[:])

        def add_to_projection(sum_ps, w_sb, n, f):
            r, h = divmod(n, N_HEAD)
            nc.tensor.matmul(
                sum_ps[:], w_sb[:, f, h * P : (h + 1) * P], x_bf[r][:, f, :],
                start=(f == 0), stop=(f == N_FBLK - 1),
            )

        def keep_q(q_ps, n):
            h = n % N_HEAD
            q_bf[n] = headpool.tile([P, SEQ], BF16, name="q_bf")
            nc.scalar.activation(q_bf[n][:], q_ps[:], IDENTITY, bias=bq_scaled[:, h : h + 1], scale=SCALE)

        def keep_k(k_ps, n, copy):
            k_bf[n] = headpool.tile([P, SEQ], BF16, name="k_bf")
            copy(k_bf[n][:], k_ps[:])

        def project_q(n):
            q_ps = wide_psum.tile([P, SEQ], F32, name="wide_ps")
            for f in range(N_FBLK):
                add_to_projection(q_ps, wq_sb, n, f)
            keep_q(q_ps, n)

        def project_k(n):
            k_ps = wide_psum.tile([P, SEQ], F32, name="wide_ps")
            for f in range(N_FBLK):
                add_to_projection(k_ps, wk_sb, n, f)
            keep_k(k_ps, n, nc.scalar.copy)

        def score_rows(n, b):
            rows = slice(b * P, (b + 1) * P)
            width = (b + 1) * P
            score = score_psum.tile([P, SEQ], F32, name="score")
            nc.tensor.matmul(score[:, :width], q_bf[n][:, rows], k_bf[n][:, :width], start=True, stop=False)
            nc.tensor.matmul(score[:, rows], identity[:], causal[:], start=False, stop=True)
            neg_max = rowpool.tile([P, 1], F32, name="neg_max")
            nc.vector.tensor_reduce(neg_max[:], score[:, :width], axis=X_AXIS, op=MAX, negate=True)
            e_f32[n, b] = rowpool.tile([P, SEQ], F32, name="e_f32")
            g, half = divmod(n, 2)
            if half == 0:
                e_sum[g, b] = rowpool.tile([P, 2], F32, name="e_sum")
            nc.scalar.activation(
                e_f32[n, b][:, :width], score[:, :width], EXP, bias=neg_max[:], scale=1.0,
                accum_out=e_sum[g, b][:, half : half + 1],
            )

        def normalise_rows(n, b):
            g, half = divmod(n, 2)
            width = (b + 1) * P
            if half == 0:
                e_inv[g, b] = rowpool.tile([P, 2], F32, name="e_inv")
                nc.vector.reciprocal(e_inv[g, b][:], e_sum[g, b][:])
            halves = p_words[g][:, b, :width].bitcast(BF16)
            nc.gpsimd.tensor_scalar(
                halves[:, half : 2 * width : 2], e_f32[n, b][:, :width], e_inv[g, b][:, half : half + 1], 0.0,
                op0=MULT, op1=ADD,
            )

        def flip_rows(g, b):
            flip = flip_psum.tile([P, N_TBLK, P], F32, name="flip")
            for t in range(b + 1):
                nc.tensor.transpose(flip[:, t, :], p_words[g][:, b, t * P : (t + 1) * P], identity_f32[:])
            nc.vector.tensor_copy(p_flip[g][:, : b + 1, b * P : (b + 1) * P], flip[:, : b + 1, :])

        def weigh_values(n, first, behind, by_vector=False):
            r, h = divmod(n, N_HEAD)
            g, half = divmod(n, 2)
            head = slice(h * P, (h + 1) * P)
            o_ps = wide_psum.tile([P, SEQ], F32, name="wide_ps")
            for t in range(behind):
                columns = slice(max(t, first) * P, behind * P)
                halves = p_flip[g][:, t, columns].bitcast(BF16)
                nc.tensor.matmul(
                    o_ps[:, columns], v_tok[r][:, t, head], halves[:, half :: 2],
                    start=(t == 0), stop=(t == behind - 1),
                )
            columns = slice(first * P, behind * P)
            o_sb = outpool.tile([P, SEQ], F32, name="o_sb")
            if by_vector:
                nc.vector.tensor_scalar_add(o_sb[:, columns], o_ps[:, columns], bv_sb[:, h : h + 1])
            else:
                nc.scalar.activation(o_sb[:, columns], o_ps[:, columns], IDENTITY, bias=bv_sb[:, h : h + 1], scale=1.0)
            nc.sync.dma_start(out[head, r * SEQ + first * P : r * SEQ + behind * P], o_sb[:, columns])

        banks = (
            [score_psum.tile([P, SEQ], F32, name="score") for bank in range(SCORE_BANKS)]
            + [flip_psum.tile([P, SEQ], F32, name="flip") for bank in range(FLIP_BANKS)]
            + [wide_psum.tile([P, SEQ], F32, name="wide_ps") for bank in range(WIDE_BANKS)]
        )
        for f in range(N_FBLK):
            for r in (0, 1):
                look_up(r, f, 0)
                look_up(r, f, 1)
            for n in range(N_HEAD):
                add_to_projection(banks[2 * n], wq_sb, n, f)
                add_to_projection(banks[2 * n + 1], wk_sb, n, f)
        for n in range(N_HEAD):
            keep_q(banks[2 * n], n)
            keep_k(banks[2 * n + 1], n, nc.vector.tensor_copy)

        last = N_PAIR - 1
        for g in range(-1, last):
            flipped = 0 <= g
            weighed = 0 <= g - 1
            p_words[g + 1] = pairpool.tile([P, N_TBLK, SEQ], F32, name="p_words")
            if flipped:
                p_flip[g] = pairpool.tile([P, N_TBLK, SEQ], F32, name="p_flip")
            for b in (3, 2, 1, 0):
                for half in (0, 1):
                    ahead = 2 * (g + 2) + half
                    if b == (3 if g >= 0 else 0) and g + 3 < N_PAIR - 2:
                        project_k(ahead + 2)
                    if b == 3 and N_PAIR - 2 <= g + 2 < N_PAIR:
                        project_k(ahead)
                    if b == 2 and g + 3 < N_PAIR:
                        project_q(ahead + 2)
                    if b == 1:
                        project_v((ahead - 2) // N_HEAD, (ahead - 2) % N_HEAD)
                    if b == 0 and weighed:
                        weigh_values(2 * (g - 1) + half, 0, N_TBLK)
                    if half == 0 and flipped:
                        flip_rows(g, b)
                    score_rows(2 * (g + 1) + half, b)
                    if b < 3:
                        normalise_rows(2 * (g + 1) + half, b + 1)
                later = 2 * (g + 5) + (N_TBLK - 1 - b) // 2
                if 2 * N_FBLK <= later < N_SEQ * N_FBLK:
                    look_up(later // N_FBLK, later % N_FBLK, (N_TBLK - 1 - b) % 2)
            normalise_rows(2 * (g + 1), 0)
            normalise_rows(2 * (g + 1) + 1, 0)

        p_flip[last] = pairpool.tile([P, N_TBLK, SEQ], F32, name="p_flip")
        for b in (3, 2, 1):
            flip_rows(last, b)
        for half in (0, 1):
            weigh_values(2 * (last - 1) + half, 0, N_TBLK)
        weigh_values(2 * last, 1, N_TBLK)
        flip_rows(last, 0)
        weigh_values(2 * last + 1, 1, N_TBLK, by_vector=True)
        weigh_values(2 * last, 0, 1)
        weigh_values(2 * last + 1, 0, 1, by_vector=True)
